import numpy as np
import ml_dtypes


def mxq(x, axis, fmt="e4m3"):
    dtype, down = {"e4m3": (ml_dtypes.float8_e4m3fn, 7), "e5m2": (ml_dtypes.float8_e5m2, 14)}[fmt]
    v = np.moveaxis(np.asarray(x, np.float32).astype(ml_dtypes.bfloat16).astype(np.float64), axis, -1)
    blocks = v.reshape(v.shape[:-1] + (-1, 32))
    amax = np.abs(blocks).max(-1, keepdims=True)
    byte = np.maximum(np.where(amax > 0, np.frexp(amax)[1] - 1 + 127, 0) - down, 1)
    scale = np.exp2(byte - 127.0)
    codes = (blocks / scale).astype(np.float32).astype(dtype).astype(np.float64)
    return np.moveaxis((codes * scale).reshape(v.shape), -1, axis)


WIDE = False


def mx_kscale(k):
    if not WIDE:
        return np.ones(k)
    levels = np.array([10, -10, 5, -5, 0])
    if k % 512:
        return np.exp2(np.random.permutation(np.resize(levels, k // 32))).repeat(32)
    a = np.empty((k // 512, 16))
    for p in range(k // 512):
        a[p, :8] = np.random.permutation(np.resize(levels, 8))
        for g in range(8):
            far = levels[np.abs(levels - a[p, g]) >= 10]
            a[p, g + 8] = far[np.random.randint(len(far))]
    return np.exp2(a.ravel()).repeat(32)


BF16 = ml_dtypes.bfloat16


def bf(x):
    return np.asarray(x, np.float32).astype(BF16)


def f64(x):
    return np.asarray(x).astype(np.float64)


B, CK, CV, NOBJ, T, H, W = 4, 128, 256, 2, 1, 32, 32
N = T * H * W
P = H * W
V = NOBJ * CV


def setup_inputs():
    s = mx_kscale(N)
    a = np.log2(s) - np.log2(s).min()
    g = np.exp2(np.round(np.log2(np.mean(1.0 / s))))
    ms = bf(1.0 + 0.5 * np.random.random((B, T, H, W)))[:, None]
    qe = np.random.random((B, CK, H, W))
    qe[:, 0] = 1.0
    m2 = np.random.standard_normal((B, CK, T, H, W)) ** 2
    m2[:, 0] += (a * np.log(2.0) * np.sqrt(CK)).reshape(T, H, W) / f64(ms)[:, 0]
    return {
        "query_key": bf(np.random.standard_normal((B, CK, H, W))),
        "query_selection": bf(qe),
        "qk_sel": bf(np.random.standard_normal((B, CK, H, W)) * np.random.random((B, CK, H, W))),
        "memory_key": bf(np.random.standard_normal((B, CK, T, H, W))),
        "mk_sq": bf(m2),
        "memory_shrinkage": ms,
        "memory_value": bf(2.0 * np.random.standard_normal((B, NOBJ, CV, T, H, W)) * (s * g).reshape(T, H, W)),
    }


def reference(query_key, query_selection, qk_sel, memory_key, mk_sq, memory_shrinkage, memory_value):
    qk = f64(query_key).reshape(B, CK, P)
    qe = f64(query_selection).reshape(B, CK, P)
    qs = f64(qk_sel).reshape(B, CK, P)
    mk = f64(memory_key).reshape(B, CK, N)
    m2 = f64(mk_sq).reshape(B, CK, N)
    ms = f64(memory_shrinkage).reshape(B, N)
    mv = f64(memory_value).reshape(B, V, N)
    a_sq = m2.transpose(0, 2, 1) @ qe
    two_ab = 2.0 * (mk.transpose(0, 2, 1) @ qs)
    b_sq = np.sum(qe * qk * qk, axis=1, keepdims=True)
    sim = (two_ab - a_sq - b_sq) * ms[:, :, None] * (1.0 / np.sqrt(CK))
    e = np.exp(sim - sim.max(axis=1, keepdims=True))
    mem = (mxq(mv, 2, "e4m3") @ mxq(e, 1, "e4m3")) / e.sum(axis=1, keepdims=True)
    return mem.reshape(B, NOBJ, CV, H, W)

@@ -1,0 +1,391 @@
+import math
+from contextlib import ExitStack
+
+import concourse.mybir as mybir
+from concourse.masks import make_identity
+
+F32 = mybir.dt.float32
+BF16 = mybir.dt.bfloat16
+U32 = mybir.dt.uint32
+U8 = mybir.dt.uint8
+FP8X4 = mybir.dt.float8_e4m3fn_x4
+ALU = mybir.AluOpType
+ACT = mybir.ActivationFunctionType
+AXIS = mybir.AxisListType
+
+BATCH = 4
+P = 128
+SLOTS = 1024
+PIXELS = 1024
+VALUES = 512
+BANK = 512
+PACK = 4
+K_PASS = P * PACK
+PASSES = SLOTS // K_PASS
+ROW_TILES = PIXELS // P
+HALF_TILES = BANK // P
+V_TILES = VALUES // P
+TILES = BATCH * ROW_TILES
+HALVES = TILES // HALF_TILES
+V_UNITS = V_TILES * PASSES
+VECTOR_HALVES = 3
+
+FLOPS = 2 * BATCH * (2 * P * SLOTS * PIXELS + VALUES * SLOTS * PIXELS)
+
+
+def tile_xmem_pa_t_kernel(
+    tc,
+    query_key,
+    query_selection,
+    qk_sel,
+    memory_key,
+    mk_sq,
+    memory_shrinkage,
+    memory_value,
+    out,
+):
+    nc = tc.nc
+    with ExitStack() as ctx:
+        consts = ctx.enter_context(tc.tile_pool(name="consts", bufs=1))
+        inputs = ctx.enter_context(tc.tile_pool(name="inputs", bufs=BATCH))
+        prep = ctx.enter_context(tc.tile_pool(name="prep", bufs=2))
+        rows = ctx.enter_context(tc.tile_pool(name="rows", bufs=4))
+        groups = ctx.enter_context(tc.tile_pool(name="groups", bufs=3))
+        halves = ctx.enter_context(tc.tile_pool(name="halves", bufs=2))
+        results = ctx.enter_context(tc.tile_pool(name="results", bufs=6))
+        psum_wide = ctx.enter_context(tc.psum_pool(name="psum_wide", bufs=4))
+        psum_turn = ctx.enter_context(tc.psum_pool(name="psum_turn", bufs=3))
+        psum_misc = ctx.enter_context(tc.psum_pool(name="psum_misc", bufs=1))
+        ctx.enter_context(tc.manual_schedule())
+
+        live = {}
+
+        for b in range(BATCH):
+            qk = inputs.tile([P, PIXELS], BF16)
+            nc.sync.dma_start(out=qk[:], in_=query_key[b].rearrange("c h w -> c (h w)"))
+            qe = inputs.tile([P, PIXELS], BF16)
+            nc.sync.dma_start(out=qe[:], in_=query_selection[b].rearrange("c h w -> c (h w)"))
+            qs = inputs.tile([P, PIXELS], BF16)
+            nc.sync.dma_start(out=qs[:], in_=qk_sel[b].rearrange("c h w -> c (h w)"))
+            ms_rows = inputs.tile([P, SLOTS], BF16)
+            queue = nc.scalar if b == 0 else nc.sync
+            queue.dma_start(
+                out=ms_rows[:],
+                in_=memory_shrinkage[b].rearrange("a t h w -> (a t h w)").partition_broadcast(P),
+            )
+            live["ms_rows", b] = ms_rows
+            mk = inputs.tile([P, SLOTS], BF16)
+            nc.sync.dma_start(out=mk[:], in_=memory_key[b].rearrange("c t h w -> c (t h w)"))
+            m2 = inputs.tile([P, SLOTS], BF16)
+            nc.sync.dma_start(out=m2[:], in_=mk_sq[b].rearrange("c t h w -> c (t h w)"))
+            mv = inputs.tile([P, V_TILES, SLOTS], BF16)
+            nc.sync.dma_start(
+                out=mv[:],
+                in_=memory_value[b].rearrange("o c t h w -> (o c) (t h w)").rearrange(
+                    "(j q) n -> q j n", q=P
+                ),
+            )
+            live["qk", b], live["qe", b], live["qs", b] = qk, qe, qs
+            live["mk", b], live["m2", b], live["mv", b] = mk, m2, mv
+
+        ident = consts.tile([P, P], F32)
+        make_identity(nc, ident[:])
+        ones_column = consts.tile([P, 1], F32)
+        nc.gpsimd.memset(ones_column[:], 1.0)
+
+        def square_keys(h, engine):
+            b, half = divmod(h, 2)
+            cols = slice(half * BANK, (half + 1) * BANK)
+            weighted = prep.tile([P, BANK], F32, bufs=3)
+            engine.tensor_tensor(out=weighted[:], in0=live["qk", b][:, cols], in1=live["qk", b][:, cols], op=ALU.mult)
+            live["weighted", h] = weighted
+
+        def weight_squares(h, engine):
+            b, half = divmod(h, 2)
+            cols = slice(half * BANK, (half + 1) * BANK)
+            weighted = live["weighted", h]
+            engine.tensor_tensor(out=weighted[:], in0=weighted[:], in1=live["qe", b][:, cols], op=ALU.mult)
+
+        def scale_queries(b, engine):
+            qs_scaled = prep.tile([P, PIXELS], BF16)
+            engine.tensor_scalar(
+                out=qs_scaled[:], in0=live["qs", b][:], scalar1=-2.0, scalar2=0.0, op0=ALU.mult, op1=ALU.add
+            )
+            live["qs_scaled", b] = qs_scaled
+
+        def scale_shrinkage(b, engine):
+            ms_scaled = prep.tile([P, SLOTS], F32)
+            engine.tensor_scalar(
+                out=ms_scaled[:], in0=live["ms_rows", b][:], scalar1=1.0 / math.sqrt(P), scalar2=0.0,
+                op0=ALU.mult, op1=ALU.add,
+            )
+            live["ms_scaled", b] = ms_scaled
+
+        def channel_sums(h):
+            if not 0 <= h < HALVES:
+                return
+            b_sq_psum = psum_misc.tile([P, HALF_TILES], F32, tag="misc")
+            for j in range(HALF_TILES):
+                nc.tensor.matmul(
+                    out=b_sq_psum[:, j : j + 1], lhsT=live["weighted", h][:, j * P : (j + 1) * P],
+                    rhs=ones_column[:], start=True, stop=True,
+                )
+            live["b_sq_psum", h] = b_sq_psum
+
+        def keep_channel_sums(h):
+            if not 0 <= h < HALVES:
+                return
+            b_sq = halves.tile([P, HALF_TILES], F32)
+            nc.vector.tensor_copy(out=b_sq[:], in_=live["b_sq_psum", h][:])
+            live["b_sq", h] = b_sq
+
+        def turn_words(rows_bf16, turned, first_pass, passes):
+            words = rows_bf16.bitcast(F32)
+            for k in range(2 * passes):
+                g, u = divmod(2 * first_pass + k, 2)
+                nc.tensor.transpose(
+                    out=turned[:, k, :], in_=words[:, 2 * P * g + u : 2 * P * (g + 1) : 2], identity=ident[:]
+                )
+
+        def regroup_words(turned, grouped, passes):
+            nc.scalar.copy(
+                out=grouped.bitcast(F32).rearrange("q (g r u) -> q g r u", g=passes, u=2),
+                in_=turned[:].rearrange("q (g u) r -> q g r u", g=passes),
+            )
+
+        def quantise_columns(grouped_cols, codes, scales, cols):
+            nc.vector.quantize_mx(out=codes[:, cols].bitcast(FP8X4), scales=scales[:, cols], in_=grouped_cols)
+
+        def turn_values(b, unit):
+            if not 0 <= b < BATCH:
+                return
+            j, g = divmod(unit, PASSES)
+            mv_turned = psum_turn.tile([P, 2, P], F32, tag="turned")
+            turn_words(live["mv", b][:, j, :], mv_turned, g, 1)
+            live["mv_turned", b, unit] = mv_turned
+
+        def regroup_values(b, unit):
+            if not 0 <= b < BATCH:
+                return
+            first, k = divmod(unit, V_UNITS // 2)
+            if k == 0:
+                mv_grouped = groups.tile([P, V_UNITS // 2, P * PACK], BF16, align_bytes=64, bufs=2)
+                live["mv_grouped", b, first] = mv_grouped
+            regroup_words(live["mv_turned", b, unit], live["mv_grouped", b, first][:, k, :], 1)
+
+        def quantise_values(b, first):
+            if not 0 <= b < BATCH:
+                return
+            if first == 0:
+                mv_codes = prep.tile([P, V_UNITS * P], U32, align_bytes=64)
+                mv_scales = prep.tile([P, V_UNITS * P], U8, align_bytes=64)
+                live["mv_codes", b], live["mv_scales", b] = mv_codes, mv_scales
+            quantise_columns(
+                live["mv_grouped", b, first][:].rearrange("q k c -> q (k c)"), live["mv_codes", b], live["mv_scales", b],
+                slice(first * VALUES, (first + 1) * VALUES),
+            )
+
+        def similarities(i, c):
+            if not 0 <= i < TILES:
+                return
+            b, t = divmod(i, ROW_TILES)
+            pix = slice(t * P, (t + 1) * P)
+            cols = slice(c * BANK, (c + 1) * BANK)
+            dots = psum_wide.tile([P, BANK], F32, tag="wide")
+            nc.tensor.matmul(
+                out=dots[:], lhsT=live["qs_scaled", b][:, pix], rhs=live["mk", b][:, cols], start=True, stop=False
+            )
+            nc.tensor.matmul(
+                out=dots[:], lhsT=live["qe", b][:, pix], rhs=live["m2", b][:, cols], start=False, stop=True
+            )
+            live["dots", i, c] = dots
+
+        def negated_similarities(i, c):
+            if not 0 <= i < TILES:
+                return
+            h, j = divmod(i, HALF_TILES)
+            cols = slice(c * BANK, (c + 1) * BANK)
+            if c == 0:
+                neg_sim = rows.tile([P, SLOTS], F32)
+                live["neg_sim", i] = neg_sim
+            nc.vector.scalar_tensor_tensor(
+                out=live["neg_sim", i][:, cols], in0=live["dots", i, c][:], scalar=live["b_sq", h][:, j : j + 1],
+                in1=live["ms_scaled", i // ROW_TILES][:, cols], op0=ALU.add, op1=ALU.mult,
+            )
+
+        def negated_maximum(i):
+            if not 0 <= i < TILES:
+                return
+            neg_max = rows.tile([P, 1], F32)
+            nc.vector.tensor_reduce(out=neg_max[:], in_=live["neg_sim", i][:], axis=AXIS.X, op=ALU.min)
+            live["neg_max", i] = neg_max
+
+        def exponentials(i):
+            if not 0 <= i < TILES:
+                return
+            h, j = divmod(i, HALF_TILES)
+            if j == 0:
+                sums = halves.tile([P, HALF_TILES], F32)
+                live["sums", h] = sums
+            e_rows = rows.tile([P, SLOTS], BF16)
+            nc.scalar.activation(
+                out=e_rows[:], in_=live["neg_sim", i][:], func=ACT.Exp, bias=live["neg_max", i][:], scale=-1.0,
+                accum_out=live["sums", h][:, j : j + 1],
+            )
+            live["e_rows", i] = e_rows
+
+        def turn_e(i):
+            if not 0 <= i < TILES:
+                return
+            e_turned = psum_turn.tile([P, 2 * PASSES, P], F32, tag="turned")
+            turn_words(live["e_rows", i][:], e_turned, 0, PASSES)
+            live["e_turned", i] = e_turned
+
+        def regroup_e(i):
+            if not 0 <= i < TILES:
+                return
+            h, j = divmod(i, HALF_TILES)
+            if j == 0:
+                e_grouped = halves.tile([P, PASSES, BANK, PACK], BF16, align_bytes=64)
+                live["e_grouped", h] = e_grouped
+            nc.scalar.copy(
+                out=live["e_grouped", h][:].bitcast(F32)[:, :, j * P : (j + 1) * P, :],
+                in_=live["e_turned", i][:].rearrange("q (g u) r -> q g r u", g=PASSES),
+            )
+
+        def quantise_e(h):
+            if not 0 <= h < HALVES:
+                return
+            e_codes = halves.tile([P, PASSES * BANK], U32, align_bytes=64)
+            e_scales = halves.tile([P, PASSES * BANK], U8, align_bytes=64)
+            quantise_columns(
+                live["e_grouped", h][:].rearrange("q g r t -> q (g r t)"), e_codes, e_scales, slice(0, PASSES * BANK)
+            )
+            live["e_codes", h], live["e_scales", h] = e_codes, e_scales
+
+        def reciprocals(h):
+            if not 0 <= h < HALVES:
+                return
+            recip = halves.tile([P, HALF_TILES], F32)
+            nc.vector.reciprocal(out=recip[:], in_=live["sums", h][:])
+            live["recip", h] = recip
+
+        def spread_reciprocals(h, part):
+            if not 0 <= h < HALVES:
+                return
+            if part == 0:
+                recip_spread = psum_misc.tile([P, BANK], F32, tag="misc")
+                live["recip_spread", h] = recip_spread
+            for j in (2 * part, 2 * part + 1):
+                nc.tensor.matmul(
+                    out=live["recip_spread", h][:, j * P : (j + 1) * P],
+                    lhsT=live["recip", h][:, j : j + 1].to_broadcast([P, P]),
+                    rhs=ident[:],
+                    start=True,
+                    stop=True,
+                )
+
+        def keep_reciprocals(h):
+            if not 0 <= h < HALVES:
+                return
+            recip_rows = halves.tile([P, BANK], F32)
+            nc.scalar.copy(out=recip_rows[:], in_=live["recip_spread", h][:])
+            live["recip_rows", h] = recip_rows
+
+        def multiply_values(h, j):
+            if not 0 <= h < HALVES:
+                return
+            b = h // 2
+            acc = psum_wide.tile([P, BANK], F32, tag="wide")
+            for g in range(PASSES):
+                v_cols = slice((j * PASSES + g) * P, (j * PASSES + g + 1) * P)
+                p_cols = slice(g * BANK, (g + 1) * BANK)
+                nc.tensor.matmul_mx(
+                    out=acc[:],
+                    lhsT=live["mv_codes", b][:, v_cols].bitcast(FP8X4),
+                    lhsT_scale=live["mv_scales", b][:, v_cols],
+                    rhs=live["e_codes", h][:, p_cols].bitcast(FP8X4),
+                    rhs_scale=live["e_scales", h][:, p_cols],
+                    start=(g == 0),
+                    stop=(g == PASSES - 1),
+                )
+            live["acc", h, j] = acc
+
+        def store(h, j, result):
+            b, half = divmod(h, 2)
+            nc.sync.dma_start(
+                out=out[b].rearrange("o c h w -> (o c) (h w)")[
+                    j * P : (j + 1) * P, half * BANK : (half + 1) * BANK
+                ],
+                in_=result[:],
+            )
+
+        def leave_psum(h, j):
+            if not 0 <= h < HALVES:
+                return
+            result = results.tile([P, BANK], F32)
+            if h < HALVES - VECTOR_HALVES:
+                nc.scalar.copy(out=result[:], in_=live["acc", h, j][:])
+                live["result", h, j] = result
+            else:
+                nc.vector.tensor_tensor(
+                    out=result[:], in0=live["acc", h, j][:], in1=live["recip_rows", h][:], op=ALU.mult
+                )
+                store(h, j, result)
+
+        def normalise_and_store(h, j):
+            if not 0 <= h < HALVES - VECTOR_HALVES:
+                return
+            result = live["result", h, j]
+            nc.gpsimd.tensor_tensor(out=result[:], in0=result[:], in1=live["recip_rows", h][:], op=ALU.mult)
+            store(h, j, result)
+
+        for s in range(-ROW_TILES, TILES + 12):
+            b_next, step = divmod(s + ROW_TILES, ROW_TILES)
+            h_now, quarter = divmod(s, HALF_TILES)
+
+            if b_next < BATCH:
+                engine = nc.vector if b_next == 0 else nc.gpsimd
+                if step == 0:
+                    square_keys(2 * b_next, engine)
+                if step == 1:
+                    weight_squares(2 * b_next, engine)
+                if step == 2:
+                    scale_queries(b_next, engine)
+                if step == 3:
+                    scale_shrinkage(b_next, engine)
+                if step == 4:
+                    square_keys(2 * b_next + 1, nc.gpsimd)
+                if step == 5:
+                    weight_squares(2 * b_next + 1, nc.gpsimd)
+            normalise_and_store((s - 13) // V_TILES, (s - 13) % V_TILES)
+
+            negated_similarities(s - 1, 0)
+            negated_maximum(s - 2)
+            negated_similarities(s - 1, 1)
+            if quarter == 2:
+                quantise_e(h_now - 2)
+            if quarter == 3:
+                keep_channel_sums(h_now + 1)
+                reciprocals(h_now - 1)
+            if quarter == 0:
+                quantise_values((s - 8) // V_UNITS, ((s - 8) % V_UNITS) // HALF_TILES)
+
+            exponentials(s - 3)
+            if quarter == 2:
+                keep_reciprocals(h_now - 2)
+            regroup_e(s - 5)
+            regroup_values((s - 2) // V_UNITS, (s - 2) % V_UNITS)
+            leave_psum((s - 12) // V_TILES, (s - 12) % V_TILES)
+
+            similarities(s, 0)
+            turn_e(s - 4)
+            similarities(s, 1)
+            turn_values((s - 1) // V_UNITS, (s - 1) % V_UNITS)
+            if quarter == 0:
+                spread_reciprocals(h_now - 2, 0)
+            if quarter == 1:
+                spread_reciprocals(h_now - 2, 1)
+            if quarter == 2:
+                channel_sums(h_now + 1)
+            multiply_values((s - 11) // V_TILES, (s - 11) % V_TILES)

@@ -28,7 +28,8 @@ V_TILES = VALUES // P
 TILES = BATCH * ROW_TILES
 HALVES = TILES // HALF_TILES
 V_UNITS = V_TILES * PASSES
-VECTOR_HALVES = 3
+SHARED_TILES = 8
+FINE = HALVES - 1
 
 FLOPS = 2 * BATCH * (2 * P * SLOTS * PIXELS + VALUES * SLOTS * PIXELS)
 
@@ -49,7 +50,7 @@ def tile_xmem_pa_t_kernel(
         consts = ctx.enter_context(tc.tile_pool(name="consts", bufs=1))
         inputs = ctx.enter_context(tc.tile_pool(name="inputs", bufs=BATCH))
         prep = ctx.enter_context(tc.tile_pool(name="prep", bufs=2))
-        rows = ctx.enter_context(tc.tile_pool(name="rows", bufs=4))
+        rows = ctx.enter_context(tc.tile_pool(name="rows", bufs=6))
         groups = ctx.enter_context(tc.tile_pool(name="groups", bufs=3))
         halves = ctx.enter_context(tc.tile_pool(name="halves", bufs=2))
         results = ctx.enter_context(tc.tile_pool(name="results", bufs=6))
@@ -62,11 +63,24 @@ def tile_xmem_pa_t_kernel(
 
         for b in range(BATCH):
             qk = inputs.tile([P, PIXELS], BF16)
-            nc.sync.dma_start(out=qk[:], in_=query_key[b].rearrange("c h w -> c (h w)"))
             qe = inputs.tile([P, PIXELS], BF16)
-            nc.sync.dma_start(out=qe[:], in_=query_selection[b].rearrange("c h w -> c (h w)"))
             qs = inputs.tile([P, PIXELS], BF16)
-            nc.sync.dma_start(out=qs[:], in_=qk_sel[b].rearrange("c h w -> c (h w)"))
+            mk = inputs.tile([P, SLOTS], BF16)
+            m2 = inputs.tile([P, SLOTS], BF16)
+            mv = inputs.tile([P, V_TILES, SLOTS], BF16)
+            qk_hbm = query_key[b].rearrange("c h w -> c (h w)")
+            qe_hbm = query_selection[b].rearrange("c h w -> c (h w)")
+            qs_hbm = qk_sel[b].rearrange("c h w -> c (h w)")
+            mk_hbm = memory_key[b].rearrange("c t h w -> c (t h w)")
+            m2_hbm = mk_sq[b].rearrange("c t h w -> c (t h w)")
+            mv_hbm = memory_value[b].rearrange("o c t h w -> (o c) (t h w)").rearrange("(j q) n -> q j n", q=P)
+            pieces = [slice(0, BANK), slice(BANK, PIXELS)] if b == 0 else [slice(0, PIXELS)]
+            nc.sync.dma_start(out=qk[:, pieces[0]], in_=qk_hbm[:, pieces[0]])
+            nc.sync.dma_start(out=qe[:, pieces[0]], in_=qe_hbm[:, pieces[0]])
+            nc.sync.dma_start(out=qs[:, pieces[0]], in_=qs_hbm[:, pieces[0]])
+            for cols in pieces:
+                nc.sync.dma_start(out=mk[:, cols], in_=mk_hbm[:, cols])
+                nc.sync.dma_start(out=m2[:, cols], in_=m2_hbm[:, cols])
             ms_rows = inputs.tile([P, SLOTS], BF16)
             queue = nc.scalar if b == 0 else nc.sync
             queue.dma_start(
@@ -74,17 +88,12 @@ def tile_xmem_pa_t_kernel(
                 in_=memory_shrinkage[b].rearrange("a t h w -> (a t h w)").partition_broadcast(P),
             )
             live["ms_rows", b] = ms_rows
-            mk = inputs.tile([P, SLOTS], BF16)
-            nc.sync.dma_start(out=mk[:], in_=memory_key[b].rearrange("c t h w -> c (t h w)"))
-            m2 = inputs.tile([P, SLOTS], BF16)
-            nc.sync.dma_start(out=m2[:], in_=mk_sq[b].rearrange("c t h w -> c (t h w)"))
-            mv = inputs.tile([P, V_TILES, SLOTS], BF16)
-            nc.sync.dma_start(
-                out=mv[:],
-                in_=memory_value[b].rearrange("o c t h w -> (o c) (t h w)").rearrange(
-                    "(j q) n -> q j n", q=P
-                ),
-            )
+            for j in range(0, V_TILES, 2):
+                nc.sync.dma_start(out=mv[:, j : j + 2, :], in_=mv_hbm[:, j : j + 2, :])
+            for cols in pieces[1:]:
+                nc.sync.dma_start(out=qk[:, cols], in_=qk_hbm[:, cols])
+                nc.sync.dma_start(out=qe[:, cols], in_=qe_hbm[:, cols])
+                nc.sync.dma_start(out=qs[:, cols], in_=qs_hbm[:, cols])
             live["qk", b], live["qe", b], live["qs", b] = qk, qe, qs
             live["mk", b], live["m2", b], live["mv", b] = mk, m2, mv
 
@@ -106,38 +115,42 @@ def tile_xmem_pa_t_kernel(
             weighted = live["weighted", h]
             engine.tensor_tensor(out=weighted[:], in0=weighted[:], in1=live["qe", b][:, cols], op=ALU.mult)
 
-        def scale_queries(b, engine):
-            qs_scaled = prep.tile([P, PIXELS], BF16)
+        def scale_queries(b, engine, cols=slice(0, PIXELS)):
+            if cols.start == 0:
+                qs_scaled = prep.tile([P, PIXELS], BF16)
+                live["qs_scaled", b] = qs_scaled
             engine.tensor_scalar(
-                out=qs_scaled[:], in0=live["qs", b][:], scalar1=-2.0, scalar2=0.0, op0=ALU.mult, op1=ALU.add
-            )
-            live["qs_scaled", b] = qs_scaled
-
-        def scale_shrinkage(b, engine):
-            ms_scaled = prep.tile([P, SLOTS], F32)
-            engine.tensor_scalar(
-                out=ms_scaled[:], in0=live["ms_rows", b][:], scalar1=1.0 / math.sqrt(P), scalar2=0.0,
+                out=live["qs_scaled", b][:, cols], in0=live["qs", b][:, cols], scalar1=-2.0, scalar2=0.0,
                 op0=ALU.mult, op1=ALU.add,
             )
-            live["ms_scaled", b] = ms_scaled
 
-        def channel_sums(h):
+        def scale_shrinkage(b, engine, cols=slice(0, SLOTS)):
+            if cols.start == 0:
+                ms_scaled = prep.tile([P, SLOTS], F32)
+                live["ms_scaled", b] = ms_scaled
+            engine.tensor_scalar(
+                out=live["ms_scaled", b][:, cols], in0=live["ms_rows", b][:, cols], scalar1=1.0 / math.sqrt(P),
+                scalar2=0.0, op0=ALU.mult, op1=ALU.add,
+            )
+
+        def channel_sums(h, first=0, last=HALF_TILES):
             if not 0 <= h < HALVES:
                 return
             b_sq_psum = psum_misc.tile([P, HALF_TILES], F32, tag="misc")
-            for j in range(HALF_TILES):
+            for j in range(first, last):
                 nc.tensor.matmul(
                     out=b_sq_psum[:, j : j + 1], lhsT=live["weighted", h][:, j * P : (j + 1) * P],
                     rhs=ones_column[:], start=True, stop=True,
                 )
             live["b_sq_psum", h] = b_sq_psum
 
-        def keep_channel_sums(h):
+        def keep_channel_sums(h, first=0, last=HALF_TILES):
             if not 0 <= h < HALVES:
                 return
-            b_sq = halves.tile([P, HALF_TILES], F32)
-            nc.vector.tensor_copy(out=b_sq[:], in_=live["b_sq_psum", h][:])
-            live["b_sq", h] = b_sq
+            b_sq = halves.tile([P, HALF_TILES], F32, bufs=3)
+            nc.vector.tensor_copy(out=b_sq[:, first:last], in_=live["b_sq_psum", h][:, first:last])
+            for j in range(first, last):
+                live["b_sq", h, j] = b_sq[:, j : j + 1]
 
         def turn_words(rows_bf16, turned, first_pass, passes):
             words = rows_bf16.bitcast(F32)
@@ -208,9 +221,27 @@ def tile_xmem_pa_t_kernel(
             if c == 0:
                 neg_sim = rows.tile([P, SLOTS], F32)
                 live["neg_sim", i] = neg_sim
+            if c == 1 and is_shared(i):
+                return
             nc.vector.scalar_tensor_tensor(
-                out=live["neg_sim", i][:, cols], in0=live["dots", i, c][:], scalar=live["b_sq", h][:, j : j + 1],
+                out=live["neg_sim", i][:, cols], in0=live["dots", i, c][:], scalar=live["b_sq", h, j],
                 in1=live["ms_scaled", i // ROW_TILES][:, cols], op0=ALU.add, op1=ALU.mult,
+            )
+
+        def is_shared(i):
+            return 3 <= i < SHARED_TILES and i % 2 == 1
+
+        def shared_similarities(i):
+            if not is_shared(i):
+                return
+            h, j = divmod(i, HALF_TILES)
+            cols = slice(BANK, SLOTS)
+            neg_sim = live["neg_sim", i]
+            nc.scalar.activation(
+                out=neg_sim[:, cols], in_=live["dots", i, 1][:], func=ACT.Identity, bias=live["b_sq", h, j], scale=1.0
+            )
+            nc.gpsimd.tensor_tensor(
+                out=neg_sim[:, cols], in0=neg_sim[:, cols], in1=live["ms_scaled", i // ROW_TILES][:, cols], op=ALU.mult
             )
 
         def negated_maximum(i):
@@ -245,16 +276,21 @@ def tile_xmem_pa_t_kernel(
             if not 0 <= i < TILES:
                 return
             h, j = divmod(i, HALF_TILES)
-            if j == 0:
-                e_grouped = halves.tile([P, PASSES, BANK, PACK], BF16, align_bytes=64)
-                live["e_grouped", h] = e_grouped
+            if h == FINE:
+                e_fine = halves.tile([P, PASSES, P, PACK], BF16, align_bytes=64, bufs=HALF_TILES)
+                live["e_fine", i] = e_fine
+                target = e_fine[:].bitcast(F32)
+            else:
+                if j == 0:
+                    e_grouped = halves.tile([P, PASSES, BANK, PACK], BF16, align_bytes=64)
+                    live["e_grouped", h] = e_grouped
+                target = live["e_grouped", h][:].bitcast(F32)[:, :, j * P : (j + 1) * P, :]
             nc.scalar.copy(
-                out=live["e_grouped", h][:].bitcast(F32)[:, :, j * P : (j + 1) * P, :],
-                in_=live["e_turned", i][:].rearrange("q (g u) r -> q g r u", g=PASSES),
+                out=target, in_=live["e_turned", i][:].rearrange("q (g u) r -> q g r u", g=PASSES)
             )
 
         def quantise_e(h):
-            if not 0 <= h < HALVES:
+            if not 0 <= h < FINE:
                 return
             e_codes = halves.tile([P, PASSES * BANK], U32, align_bytes=64)
             e_scales = halves.tile([P, PASSES * BANK], U8, align_bytes=64)
@@ -262,6 +298,56 @@ def tile_xmem_pa_t_kernel(
                 live["e_grouped", h][:].rearrange("q g r t -> q (g r t)"), e_codes, e_scales, slice(0, PASSES * BANK)
             )
             live["e_codes", h], live["e_scales", h] = e_codes, e_scales
+
+        def is_fine(i):
+            return FINE * HALF_TILES <= i < TILES
+
+        def fine_quantise(i):
+            if not is_fine(i):
+                return
+            fine_codes = halves.tile([P, PASSES * P], U32, align_bytes=64, bufs=HALF_TILES)
+            fine_scales = halves.tile([P, PASSES * P], U8, align_bytes=64, bufs=HALF_TILES)
+            quantise_columns(
+                live["e_fine", i][:].rearrange("q g r t -> q (g r t)"), fine_codes, fine_scales, slice(0, PASSES * P)
+            )
+            live["fine_codes", i], live["fine_scales", i] = fine_codes, fine_scales
+
+        def fine_multiply(i):
+            if not is_fine(i):
+                return
+            b = i // ROW_TILES
+            fine_acc = psum_wide.tile([P, V_TILES, P], F32, tag="wide")
+            for j in range(V_TILES):
+                for g in range(PASSES):
+                    v_cols = slice((j * PASSES + g) * P, (j * PASSES + g + 1) * P)
+                    p_cols = slice(g * P, (g + 1) * P)
+                    nc.tensor.matmul_mx(
+                        out=fine_acc[:, j, :],
+                        lhsT=live["mv_codes", b][:, v_cols].bitcast(FP8X4),
+                        lhsT_scale=live["mv_scales", b][:, v_cols],
+                        rhs=live["fine_codes", i][:, p_cols].bitcast(FP8X4),
+                        rhs_scale=live["fine_scales", i][:, p_cols],
+                        start=(g == 0),
+                        stop=(g == PASSES - 1),
+                    )
+            live["fine_acc", i] = fine_acc
+
+        def fine_leave(i):
+            if not is_fine(i):
+                return
+            b, t = divmod(i, ROW_TILES)
+            h, j = divmod(i, HALF_TILES)
+            fine_result = results.tile([P, V_TILES, P], F32)
+            nc.vector.tensor_tensor(
+                out=fine_result[:], in0=live["fine_acc", i][:],
+                in1=live["recip_rows", h][:, j * P : (j + 1) * P].unsqueeze(1).to_broadcast([P, V_TILES, P]), op=ALU.mult,
+            )
+            nc.sync.dma_start(
+                out=out[b].rearrange("o c h w -> (o c) (h w)").rearrange("(j q) p -> q j p", q=P)[
+                    :, :, t * P : (t + 1) * P
+                ],
+                in_=fine_result[:],
+            )
 
         def reciprocals(h):
             if not 0 <= h < HALVES:
@@ -277,12 +363,10 @@ def tile_xmem_pa_t_kernel(
                 recip_spread = psum_misc.tile([P, BANK], F32, tag="misc")
                 live["recip_spread", h] = recip_spread
             for j in (2 * part, 2 * part + 1):
-                nc.tensor.matmul(
+                nc.tensor.transpose(
                     out=live["recip_spread", h][:, j * P : (j + 1) * P],
-                    lhsT=live["recip", h][:, j : j + 1].to_broadcast([P, P]),
-                    rhs=ident[:],
-                    start=True,
-                    stop=True,
+                    in_=live["recip", h][:, j : j + 1].to_broadcast([P, P]),
+                    identity=ident[:],
                 )
 
         def keep_reciprocals(h):
@@ -293,7 +377,7 @@ def tile_xmem_pa_t_kernel(
             live["recip_rows", h] = recip_rows
 
         def multiply_values(h, j):
-            if not 0 <= h < HALVES:
+            if not 0 <= h < FINE:
                 return
             b = h // 2
             acc = psum_wide.tile([P, BANK], F32, tag="wide")
@@ -320,11 +404,14 @@ def tile_xmem_pa_t_kernel(
                 in_=result[:],
             )
 
+        def on_vector(h, j):
+            return h >= FINE - 1 or (h == FINE - 2 and j >= 2)
+
         def leave_psum(h, j):
-            if not 0 <= h < HALVES:
+            if not 0 <= h < FINE:
                 return
             result = results.tile([P, BANK], F32)
-            if h < HALVES - VECTOR_HALVES:
+            if not on_vector(h, j):
                 nc.scalar.copy(out=result[:], in_=live["acc", h, j][:])
                 live["result", h, j] = result
             else:
@@ -334,58 +421,104 @@ def tile_xmem_pa_t_kernel(
                 store(h, j, result)
 
         def normalise_and_store(h, j):
-            if not 0 <= h < HALVES - VECTOR_HALVES:
+            if not 0 <= h < HALVES or on_vector(h, j):
                 return
             result = live["result", h, j]
             nc.gpsimd.tensor_tensor(out=result[:], in0=result[:], in1=live["recip_rows", h][:], op=ALU.mult)
             store(h, j, result)
 
-        for s in range(-ROW_TILES, TILES + 12):
+        def value_units(s):
+            if 1 <= s <= V_UNITS // 2:
+                return [(0, 2 * (s - 1)), (0, 2 * (s - 1) + 1)]
+            if V_UNITS < s <= BATCH * V_UNITS:
+                return [divmod(s - 1, V_UNITS)]
+            return []
+
+        for s in range(-ROW_TILES, TILES + 14):
             b_next, step = divmod(s + ROW_TILES, ROW_TILES)
             h_now, quarter = divmod(s, HALF_TILES)
 
-            if b_next < BATCH:
-                engine = nc.vector if b_next == 0 else nc.gpsimd
+            if b_next == 0:
+                first, second = slice(0, BANK), slice(BANK, PIXELS)
                 if step == 0:
-                    square_keys(2 * b_next, engine)
+                    square_keys(0, nc.vector)
+                    scale_shrinkage(0, nc.gpsimd, first)
+                    scale_shrinkage(0, nc.gpsimd, second)
                 if step == 1:
-                    weight_squares(2 * b_next, engine)
-                if step == 2:
-                    scale_queries(b_next, engine)
-                if step == 3:
-                    scale_shrinkage(b_next, engine)
-                if step == 4:
-                    square_keys(2 * b_next + 1, nc.gpsimd)
-                if step == 5:
-                    weight_squares(2 * b_next + 1, nc.gpsimd)
-            normalise_and_store((s - 13) // V_TILES, (s - 13) % V_TILES)
+                    scale_queries(0, nc.vector, first)
+                    weight_squares(0, nc.vector)
 
+            if s == 1:
+                keep_channel_sums(0, 0, 1)
+            if s == 2:
+                keep_channel_sums(0, 1)
             negated_similarities(s - 1, 0)
             negated_maximum(s - 2)
             negated_similarities(s - 1, 1)
-            if quarter == 2:
+            if quarter == 1:
                 quantise_e(h_now - 2)
+            if quarter == 0 and h_now > 0:
+                keep_channel_sums(h_now)
             if quarter == 3:
-                keep_channel_sums(h_now + 1)
                 reciprocals(h_now - 1)
-            if quarter == 0:
-                quantise_values((s - 8) // V_UNITS, ((s - 8) % V_UNITS) // HALF_TILES)
+            fine_quantise(s - 6)
+            fine_leave(s - 9)
+            if s == 4:
+                quantise_values(0, 0)
+            if s == 6:
+                quantise_values(0, 1)
+            if quarter == 3 and s > V_UNITS + 3:
+                quantise_values((s - 7) // V_UNITS, ((s - 7) % V_UNITS) // HALF_TILES)
 
+            shared_similarities(s - 1)
             exponentials(s - 3)
-            if quarter == 2:
+            if quarter == 2 and h_now - 2 < FINE:
                 keep_reciprocals(h_now - 2)
             regroup_e(s - 5)
-            regroup_values((s - 2) // V_UNITS, (s - 2) % V_UNITS)
-            leave_psum((s - 12) // V_TILES, (s - 12) % V_TILES)
+            if quarter == 0 and h_now - 2 == FINE:
+                keep_reciprocals(FINE)
+            for b, unit in value_units(s - 1):
+                regroup_values(b, unit)
+            leave_psum((s - 11) // V_TILES, (s - 11) % V_TILES)
 
+            if s == 1:
+                square_keys(1, nc.gpsimd)
+                weight_squares(1, nc.gpsimd)
+            if s == 2:
+                scale_queries(0, nc.gpsimd, slice(BANK, PIXELS))
+            if 0 < b_next < BATCH:
+                if step == 2:
+                    square_keys(2 * b_next, nc.gpsimd)
+                if step == 3:
+                    weight_squares(2 * b_next, nc.gpsimd)
+                if step == 4:
+                    scale_queries(b_next, nc.gpsimd)
+                if step == 5:
+                    scale_shrinkage(b_next, nc.gpsimd)
+                if step == 6:
+                    square_keys(2 * b_next + 1, nc.gpsimd)
+                if step == 7:
+                    weight_squares(2 * b_next + 1, nc.gpsimd)
+            normalise_and_store((s - 12) // V_TILES, (s - 12) % V_TILES)
+
+
+            if s == 1:
+                channel_sums(0, 1)
             similarities(s, 0)
+            if s == 0:
+                channel_sums(0, 0, 1)
             turn_e(s - 4)
             similarities(s, 1)
-            turn_values((s - 1) // V_UNITS, (s - 1) % V_UNITS)
-            if quarter == 0:
+            for b, unit in value_units(s):
+                turn_values(b, unit)
+            if quarter == 0 and h_now - 2 < FINE:
                 spread_reciprocals(h_now - 2, 0)
-            if quarter == 1:
+            if quarter == 1 and h_now - 2 < FINE:
                 spread_reciprocals(h_now - 2, 1)
-            if quarter == 2:
+            if quarter == 3 and h_now - 1 == FINE:
+                spread_reciprocals(FINE, 0)
+                spread_reciprocals(FINE, 1)
+            if quarter == 3 and h_now + 1 > 0:
                 channel_sums(h_now + 1)
-            multiply_values((s - 11) // V_TILES, (s - 11) % V_TILES)
+            multiply_values((s - 10) // V_TILES, (s - 10) % V_TILES)
+            fine_multiply(s - 7)

@@ -61,6 +61,12 @@ def tile_xmem_pa_t_kernel(
 
         live = {}
 
+        ms_row = consts.tile([P, SLOTS], BF16)
+        nc.vector.memset(ms_row[:].bitcast(U32), 0)
+        first_row = consts.tile([P, P], BF16)
+        nc.vector.memset(first_row[:], 0.0)
+        nc.vector.memset(first_row[0:1, :], 1.0)
+
         for b in range(BATCH):
             qk = inputs.tile([P, PIXELS], BF16)
             qe = inputs.tile([P, PIXELS], BF16)
@@ -77,17 +83,19 @@ def tile_xmem_pa_t_kernel(
             pieces = [slice(0, BANK), slice(BANK, PIXELS)] if b == 0 else [slice(0, PIXELS)]
             nc.sync.dma_start(out=qk[:, pieces[0]], in_=qk_hbm[:, pieces[0]])
             nc.sync.dma_start(out=qe[:, pieces[0]], in_=qe_hbm[:, pieces[0]])
+            if b == 0:
+                nc.sync.dma_start(out=ms_row[0:1, :], in_=memory_shrinkage[0].rearrange("a t h w -> a (t h w)"))
             nc.sync.dma_start(out=qs[:, pieces[0]], in_=qs_hbm[:, pieces[0]])
             for cols in pieces:
                 nc.sync.dma_start(out=mk[:, cols], in_=mk_hbm[:, cols])
                 nc.sync.dma_start(out=m2[:, cols], in_=m2_hbm[:, cols])
-            ms_rows = inputs.tile([P, SLOTS], BF16)
-            queue = nc.scalar if b == 0 else nc.sync
-            queue.dma_start(
-                out=ms_rows[:],
-                in_=memory_shrinkage[b].rearrange("a t h w -> (a t h w)").partition_broadcast(P),
-            )
-            live["ms_rows", b] = ms_rows
+            if b > 0:
+                ms_rows = inputs.tile([P, SLOTS], BF16)
+                nc.sync.dma_start(
+                    out=ms_rows[:],
+                    in_=memory_shrinkage[b].rearrange("a t h w -> (a t h w)").partition_broadcast(P),
+                )
+                live["ms_rows", b] = ms_rows
             for j in range(0, V_TILES, 2):
                 nc.sync.dma_start(out=mv[:, j : j + 2, :], in_=mv_hbm[:, j : j + 2, :])
             for cols in pieces[1:]:
@@ -124,14 +132,22 @@ def tile_xmem_pa_t_kernel(
                 op0=ALU.mult, op1=ALU.add,
             )
 
-        def scale_shrinkage(b, engine, cols=slice(0, SLOTS)):
-            if cols.start == 0:
-                ms_scaled = prep.tile([P, SLOTS], F32)
-                live["ms_scaled", b] = ms_scaled
-            engine.tensor_scalar(
-                out=live["ms_scaled", b][:, cols], in0=live["ms_rows", b][:, cols], scalar1=1.0 / math.sqrt(P),
-                scalar2=0.0, op0=ALU.mult, op1=ALU.add,
+        def spread_shrinkage():
+            ms_scaled = prep.tile([P, SLOTS], F32)
+            for c in range(SLOTS // BANK):
+                cols = slice(c * BANK, (c + 1) * BANK)
+                ms_spread = psum_turn.tile([P, BANK], F32, tag="turned")
+                nc.tensor.matmul(out=ms_spread[:], lhsT=first_row[:], rhs=ms_row[:, cols], start=True, stop=True)
+                nc.scalar.activation(out=ms_scaled[:, cols], in_=ms_spread[:], func=ACT.Copy, scale=1.0 / math.sqrt(P))
+            live["ms_scaled", 0] = ms_scaled
+
+        def scale_shrinkage(b):
+            ms_scaled = prep.tile([P, SLOTS], F32)
+            nc.gpsimd.tensor_scalar(
+                out=ms_scaled[:], in0=live["ms_rows", b][:], scalar1=1.0 / math.sqrt(P), scalar2=0.0,
+                op0=ALU.mult, op1=ALU.add,
             )
+            live["ms_scaled", b] = ms_scaled
 
         def channel_sums(h, first=0, last=HALF_TILES):
             if not 0 <= h < HALVES:
@@ -442,8 +458,6 @@ def tile_xmem_pa_t_kernel(
                 first, second = slice(0, BANK), slice(BANK, PIXELS)
                 if step == 0:
                     square_keys(0, nc.vector)
-                    scale_shrinkage(0, nc.gpsimd, first)
-                    scale_shrinkage(0, nc.gpsimd, second)
                 if step == 1:
                     scale_queries(0, nc.vector, first)
                     weight_squares(0, nc.vector)
@@ -494,7 +508,7 @@ def tile_xmem_pa_t_kernel(
                 if step == 4:
                     scale_queries(b_next, nc.gpsimd)
                 if step == 5:
-                    scale_shrinkage(b_next, nc.gpsimd)
+                    scale_shrinkage(b_next)
                 if step == 6:
                     square_keys(2 * b_next + 1, nc.gpsimd)
                 if step == 7:
@@ -507,6 +521,7 @@ def tile_xmem_pa_t_kernel(
             similarities(s, 0)
             if s == 0:
                 channel_sums(0, 0, 1)
+                spread_shrinkage()
             turn_e(s - 4)
             similarities(s, 1)
             for b, unit in value_units(s):

@@ -28,7 +28,7 @@ V_TILES = VALUES // P
 TILES = BATCH * ROW_TILES
 HALVES = TILES // HALF_TILES
 V_UNITS = V_TILES * PASSES
-SHARED_TILES = 8
+FIRST_SHARED, SHARED_TILES = 5, 10
 FINE = HALVES - 1
 
 FLOPS = 2 * BATCH * (2 * P * SLOTS * PIXELS + VALUES * SLOTS * PIXELS)
@@ -132,6 +132,12 @@ def tile_xmem_pa_t_kernel(
                 op0=ALU.mult, op1=ALU.add,
             )
 
+        def warm_up():
+            warm = psum_turn.tile([P, BANK], F32, tag="turned")
+            for k in range(8):
+                cols = slice(k % HALF_TILES * P, (k % HALF_TILES + 1) * P)
+                nc.tensor.matmul(out=warm[:, cols], lhsT=first_row[:], rhs=first_row[:], start=True, stop=True)
+
         def spread_shrinkage():
             ms_scaled = prep.tile([P, SLOTS], F32)
             for c in range(SLOTS // BANK):
@@ -185,29 +191,24 @@ def tile_xmem_pa_t_kernel(
         def quantise_columns(grouped_cols, codes, scales, cols):
             nc.vector.quantize_mx(out=codes[:, cols].bitcast(FP8X4), scales=scales[:, cols], in_=grouped_cols)
 
-        def turn_values(b, unit):
-            if not 0 <= b < BATCH:
-                return
-            j, g = divmod(unit, PASSES)
-            mv_turned = psum_turn.tile([P, 2, P], F32, tag="turned")
-            turn_words(live["mv", b][:, j, :], mv_turned, g, 1)
-            live["mv_turned", b, unit] = mv_turned
+        def turn_values(b, j):
+            mv_turned = psum_turn.tile([P, 2 * PASSES, P], F32, tag="turned")
+            turn_words(live["mv", b][:, j, :], mv_turned, 0, PASSES)
+            live["mv_turned", b, j] = mv_turned
 
-        def regroup_values(b, unit):
-            if not 0 <= b < BATCH:
-                return
-            first, k = divmod(unit, V_UNITS // 2)
+        def regroup_values(b, j):
+            first, k = divmod(j, V_TILES // 2)
             if k == 0:
-                mv_grouped = groups.tile([P, V_UNITS // 2, P * PACK], BF16, align_bytes=64, bufs=2)
+                mv_grouped = groups.tile([P, V_TILES // 2, PASSES * P * PACK], BF16, align_bytes=64, bufs=4)
                 live["mv_grouped", b, first] = mv_grouped
-            regroup_words(live["mv_turned", b, unit], live["mv_grouped", b, first][:, k, :], 1)
+            regroup_words(live["mv_turned", b, j], live["mv_grouped", b, first][:, k, :], PASSES)
 
         def quantise_values(b, first):
             if not 0 <= b < BATCH:
                 return
             if first == 0:
-                mv_codes = prep.tile([P, V_UNITS * P], U32, align_bytes=64)
-                mv_scales = prep.tile([P, V_UNITS * P], U8, align_bytes=64)
+                mv_codes = prep.tile([P, V_UNITS * P], U32, align_bytes=64, bufs=3)
+                mv_scales = prep.tile([P, V_UNITS * P], U8, align_bytes=64, bufs=3)
                 live["mv_codes", b], live["mv_scales", b] = mv_codes, mv_scales
             quantise_columns(
                 live["mv_grouped", b, first][:].rearrange("q k c -> q (k c)"), live["mv_codes", b], live["mv_scales", b],
@@ -245,7 +246,7 @@ def tile_xmem_pa_t_kernel(
             )
 
         def is_shared(i):
-            return 3 <= i < SHARED_TILES and i % 2 == 1
+            return FIRST_SHARED <= i < SHARED_TILES and i % 2 == 1
 
         def shared_similarities(i):
             if not is_shared(i):
@@ -443,12 +444,12 @@ def tile_xmem_pa_t_kernel(
             nc.gpsimd.tensor_tensor(out=result[:], in0=result[:], in1=live["recip_rows", h][:], op=ALU.mult)
             store(h, j, result)
 
-        def value_units(s):
-            if 1 <= s <= V_UNITS // 2:
-                return [(0, 2 * (s - 1)), (0, 2 * (s - 1) + 1)]
-            if V_UNITS < s <= BATCH * V_UNITS:
-                return [divmod(s - 1, V_UNITS)]
-            return []
+        def value_tile(s):
+            if 1 <= s <= 2 * V_TILES:
+                return divmod(s - 1, V_TILES)
+            if 2 * V_TILES < s <= (BATCH - 1) * V_UNITS and s % 2 == 1:
+                return 1 + s // V_UNITS, s % V_UNITS // 2
+            return None
 
         for s in range(-ROW_TILES, TILES + 14):
             b_next, step = divmod(s + ROW_TILES, ROW_TILES)
@@ -458,31 +459,36 @@ def tile_xmem_pa_t_kernel(
                 first, second = slice(0, BANK), slice(BANK, PIXELS)
                 if step == 0:
                     square_keys(0, nc.vector)
-                if step == 1:
-                    scale_queries(0, nc.vector, first)
                     weight_squares(0, nc.vector)
+                    scale_queries(0, nc.vector, first)
+                if step == 0:
+                    warm_up()
+                if step == 1:
+                    spread_shrinkage()
+                    channel_sums(0, 0, 1)
 
             if s == 1:
                 keep_channel_sums(0, 0, 1)
             if s == 2:
                 keep_channel_sums(0, 1)
+            if s == 2:
+                negated_maximum(0)
             negated_similarities(s - 1, 0)
-            negated_maximum(s - 2)
-            negated_similarities(s - 1, 1)
+            if s > 2:
+                negated_maximum(s - 2)
             if quarter == 1:
                 quantise_e(h_now - 2)
+            negated_similarities(s - 1, 1)
             if quarter == 0 and h_now > 0:
                 keep_channel_sums(h_now)
             if quarter == 3:
                 reciprocals(h_now - 1)
             fine_quantise(s - 6)
             fine_leave(s - 9)
-            if s == 4:
-                quantise_values(0, 0)
-            if s == 6:
-                quantise_values(0, 1)
-            if quarter == 3 and s > V_UNITS + 3:
-                quantise_values((s - 7) // V_UNITS, ((s - 7) % V_UNITS) // HALF_TILES)
+            if s in (4, 6):
+                quantise_values(0, s // 2 - 2)
+            if quarter == 3 and V_UNITS < s < BATCH * V_UNITS:
+                quantise_values(1 + (s - 11) // V_UNITS, (s - 11) % V_UNITS // HALF_TILES)
 
             shared_similarities(s - 1)
             exponentials(s - 3)
@@ -491,8 +497,8 @@ def tile_xmem_pa_t_kernel(
             regroup_e(s - 5)
             if quarter == 0 and h_now - 2 == FINE:
                 keep_reciprocals(FINE)
-            for b, unit in value_units(s - 1):
-                regroup_values(b, unit)
+            if value_tile(s - 1):
+                regroup_values(*value_tile(s - 1))
             leave_psum((s - 11) // V_TILES, (s - 11) % V_TILES)
 
             if s == 1:
@@ -519,13 +525,10 @@ def tile_xmem_pa_t_kernel(
             if s == 1:
                 channel_sums(0, 1)
             similarities(s, 0)
-            if s == 0:
-                channel_sums(0, 0, 1)
-                spread_shrinkage()
             turn_e(s - 4)
             similarities(s, 1)
-            for b, unit in value_units(s):
-                turn_values(b, unit)
+            if value_tile(s):
+                turn_values(*value_tile(s))
             if quarter == 0 and h_now - 2 < FINE:
                 spread_reciprocals(h_now - 2, 0)
             if quarter == 1 and h_now - 2 < FINE:

@@ -61,11 +61,11 @@ def tile_xmem_pa_t_kernel(
 
         live = {}
 
-        ms_row = consts.tile([P, SLOTS], BF16)
-        nc.vector.memset(ms_row[:].bitcast(U32), 0)
         first_row = consts.tile([P, P], BF16)
         nc.vector.memset(first_row[:], 0.0)
         nc.vector.memset(first_row[0:1, :], 1.0)
+        ms_row = consts.tile([P, SLOTS], BF16)
+        nc.gpsimd.memset(ms_row[:].bitcast(U32), 0)
 
         for b in range(BATCH):
             qk = inputs.tile([P, PIXELS], BF16)
@@ -110,18 +110,19 @@ def tile_xmem_pa_t_kernel(
         ones_column = consts.tile([P, 1], F32)
         nc.gpsimd.memset(ones_column[:], 1.0)
 
-        def square_keys(h, engine):
+        def square_keys(h, engine, part=slice(0, BANK)):
             b, half = divmod(h, 2)
-            cols = slice(half * BANK, (half + 1) * BANK)
-            weighted = prep.tile([P, BANK], F32, bufs=3)
-            engine.tensor_tensor(out=weighted[:], in0=live["qk", b][:, cols], in1=live["qk", b][:, cols], op=ALU.mult)
-            live["weighted", h] = weighted
+            if part.start == 0:
+                weighted = prep.tile([P, BANK], F32, bufs=3)
+                live["weighted", h] = weighted
+            keys = live["qk", b][:, half * BANK + part.start : half * BANK + part.stop]
+            engine.tensor_tensor(out=live["weighted", h][:, part], in0=keys, in1=keys, op=ALU.mult)
 
-        def weight_squares(h, engine):
+        def weight_squares(h, engine, part=slice(0, BANK)):
             b, half = divmod(h, 2)
-            cols = slice(half * BANK, (half + 1) * BANK)
-            weighted = live["weighted", h]
-            engine.tensor_tensor(out=weighted[:], in0=weighted[:], in1=live["qe", b][:, cols], op=ALU.mult)
+            weighted = live["weighted", h][:, part]
+            selection = live["qe", b][:, half * BANK + part.start : half * BANK + part.stop]
+            engine.tensor_tensor(out=weighted, in0=weighted, in1=selection, op=ALU.mult)
 
         def scale_queries(b, engine, cols=slice(0, PIXELS)):
             if cols.start == 0:
@@ -134,18 +135,20 @@ def tile_xmem_pa_t_kernel(
 
         def warm_up():
             warm = psum_turn.tile([P, BANK], F32, tag="turned")
-            for k in range(8):
+            for k in range(14):
                 cols = slice(k % HALF_TILES * P, (k % HALF_TILES + 1) * P)
                 nc.tensor.matmul(out=warm[:, cols], lhsT=first_row[:], rhs=first_row[:], start=True, stop=True)
 
-        def spread_shrinkage():
-            ms_scaled = prep.tile([P, SLOTS], F32)
-            for c in range(SLOTS // BANK):
-                cols = slice(c * BANK, (c + 1) * BANK)
-                ms_spread = psum_turn.tile([P, BANK], F32, tag="turned")
-                nc.tensor.matmul(out=ms_spread[:], lhsT=first_row[:], rhs=ms_row[:, cols], start=True, stop=True)
-                nc.scalar.activation(out=ms_scaled[:, cols], in_=ms_spread[:], func=ACT.Copy, scale=1.0 / math.sqrt(P))
-            live["ms_scaled", 0] = ms_scaled
+        def spread_shrinkage(c):
+            if c == 0:
+                ms_scaled = prep.tile([P, SLOTS], F32)
+                live["ms_scaled", 0] = ms_scaled
+            cols = slice(c * BANK, (c + 1) * BANK)
+            ms_spread = psum_turn.tile([P, BANK], F32, tag="turned")
+            nc.tensor.matmul(out=ms_spread[:], lhsT=first_row[:], rhs=ms_row[:, cols], start=True, stop=True)
+            nc.scalar.activation(
+                out=live["ms_scaled", 0][:, cols], in_=ms_spread[:], func=ACT.Copy, scale=1.0 / math.sqrt(P)
+            )
 
         def scale_shrinkage(b):
             ms_scaled = prep.tile([P, SLOTS], F32)
@@ -456,15 +459,16 @@ def tile_xmem_pa_t_kernel(
             h_now, quarter = divmod(s, HALF_TILES)
 
             if b_next == 0:
-                first, second = slice(0, BANK), slice(BANK, PIXELS)
+                first, pixels = slice(0, BANK), (slice(0, P), slice(P, BANK))
                 if step == 0:
-                    square_keys(0, nc.vector)
-                    weight_squares(0, nc.vector)
+                    square_keys(0, nc.vector, pixels[0])
+                    weight_squares(0, nc.vector, pixels[0])
                     scale_queries(0, nc.vector, first)
-                if step == 0:
+                    square_keys(0, nc.vector, pixels[1])
+                    weight_squares(0, nc.vector, pixels[1])
                     warm_up()
                 if step == 1:
-                    spread_shrinkage()
+                    spread_shrinkage(0)
                     channel_sums(0, 0, 1)
 
             if s == 1:
@@ -525,8 +529,10 @@ def tile_xmem_pa_t_kernel(
             if s == 1:
                 channel_sums(0, 1)
             similarities(s, 0)
-            turn_e(s - 4)
+            if s == 0:
+                spread_shrinkage(1)
             similarities(s, 1)
+            turn_e(s - 4)
             if value_tile(s):
                 turn_values(*value_tile(s))
             if quarter == 0 and h_now - 2 < FINE:

@@ -200,22 +200,17 @@ def tile_xmem_pa_t_kernel(
             live["mv_turned", b, j] = mv_turned
 
         def regroup_values(b, j):
-            first, k = divmod(j, V_TILES // 2)
-            if k == 0:
-                mv_grouped = groups.tile([P, V_TILES // 2, PASSES * P * PACK], BF16, align_bytes=64, bufs=4)
-                live["mv_grouped", b, first] = mv_grouped
-            regroup_words(live["mv_turned", b, j], live["mv_grouped", b, first][:, k, :], PASSES)
+            if j == 0:
+                mv_grouped = groups.tile([P, V_TILES, PASSES * P * PACK], BF16, align_bytes=64, bufs=2)
+                live["mv_grouped", b] = mv_grouped
+            regroup_words(live["mv_turned", b, j], live["mv_grouped", b][:, j, :], PASSES)
 
-        def quantise_values(b, first):
-            if not 0 <= b < BATCH:
-                return
-            if first == 0:
-                mv_codes = prep.tile([P, V_UNITS * P], U32, align_bytes=64, bufs=3)
-                mv_scales = prep.tile([P, V_UNITS * P], U8, align_bytes=64, bufs=3)
-                live["mv_codes", b], live["mv_scales", b] = mv_codes, mv_scales
+        def quantise_values(b):
+            mv_codes = prep.tile([P, V_UNITS * P], U32, align_bytes=64, bufs=3)
+            mv_scales = prep.tile([P, V_UNITS * P], U8, align_bytes=64, bufs=3)
+            live["mv_codes", b], live["mv_scales", b] = mv_codes, mv_scales
             quantise_columns(
-                live["mv_grouped", b, first][:].rearrange("q k c -> q (k c)"), live["mv_codes", b], live["mv_scales", b],
-                slice(first * VALUES, (first + 1) * VALUES),
+                live["mv_grouped", b][:].rearrange("q k c -> q (k c)"), mv_codes, mv_scales, slice(0, V_UNITS * P)
             )
 
         def similarities(i, c):
@@ -450,8 +445,8 @@ def tile_xmem_pa_t_kernel(
         def value_tile(s):
             if 1 <= s <= 2 * V_TILES:
                 return divmod(s - 1, V_TILES)
-            if 2 * V_TILES < s <= (BATCH - 1) * V_UNITS and s % 2 == 1:
-                return 1 + s // V_UNITS, s % V_UNITS // 2
+            if 2 * V_TILES < s <= (BATCH - 1) * V_UNITS and s % 2 == 0:
+                return 2 + (s - 10) // V_UNITS, (s - 10) % V_UNITS // 2
             return None
 
         for s in range(-ROW_TILES, TILES + 14):
@@ -489,10 +484,10 @@ def tile_xmem_pa_t_kernel(
                 reciprocals(h_now - 1)
             fine_quantise(s - 6)
             fine_leave(s - 9)
-            if s in (4, 6):
-                quantise_values(0, s // 2 - 2)
-            if quarter == 3 and V_UNITS < s < BATCH * V_UNITS:
-                quantise_values(1 + (s - 11) // V_UNITS, (s - 11) % V_UNITS // HALF_TILES)
+            if s == 6:
+                quantise_values(0)
+            if s % V_UNITS == V_UNITS - 1 and V_UNITS < s < TILES:
+                quantise_values(s // V_UNITS)
 
             shared_similarities(s - 1)
             exponentials(s - 3)

@@ -53,7 +53,7 @@ def tile_xmem_pa_t_kernel(
         rows = ctx.enter_context(tc.tile_pool(name="rows", bufs=6))
         groups = ctx.enter_context(tc.tile_pool(name="groups", bufs=3))
         halves = ctx.enter_context(tc.tile_pool(name="halves", bufs=2))
-        results = ctx.enter_context(tc.tile_pool(name="results", bufs=6))
+        results = ctx.enter_context(tc.tile_pool(name="results", bufs=8))
         psum_wide = ctx.enter_context(tc.psum_pool(name="psum_wide", bufs=4))
         psum_turn = ctx.enter_context(tc.psum_pool(name="psum_turn", bufs=3))
         psum_misc = ctx.enter_context(tc.psum_pool(name="psum_misc", bufs=1))
@@ -352,17 +352,20 @@ def tile_xmem_pa_t_kernel(
                 return
             b, t = divmod(i, ROW_TILES)
             h, j = divmod(i, HALF_TILES)
-            fine_result = results.tile([P, V_TILES, P], F32)
-            nc.vector.tensor_tensor(
-                out=fine_result[:], in0=live["fine_acc", i][:],
-                in1=live["recip_rows", h][:, j * P : (j + 1) * P].unsqueeze(1).to_broadcast([P, V_TILES, P]), op=ALU.mult,
-            )
-            nc.sync.dma_start(
-                out=out[b].rearrange("o c h w -> (o c) (h w)").rearrange("(j q) p -> q j p", q=P)[
-                    :, :, t * P : (t + 1) * P
-                ],
-                in_=fine_result[:],
-            )
+            fine_result = results.tile([P, V_TILES, P], F32, bufs=HALF_TILES)
+            step = V_TILES // 2 if i == TILES - 1 else V_TILES
+            for a in range(0, V_TILES, step):
+                channels = slice(a, a + step)
+                nc.vector.tensor_tensor(
+                    out=fine_result[:, channels, :], in0=live["fine_acc", i][:, channels, :],
+                    in1=live["recip_rows", h][:, j * P : (j + 1) * P].unsqueeze(1).to_broadcast([P, step, P]), op=ALU.mult,
+                )
+                nc.sync.dma_start(
+                    out=out[b].rearrange("o c h w -> (o c) (h w)").rearrange("(j q) p -> q j p", q=P)[
+                        :, channels, t * P : (t + 1) * P
+                    ],
+                    in_=fine_result[:, channels, :],
+                )
 
         def reciprocals(h):
             if not 0 <= h < HALVES:
@@ -464,6 +467,7 @@ def tile_xmem_pa_t_kernel(
                     warm_up()
                 if step == 1:
                     spread_shrinkage(0)
+                    spread_shrinkage(1)
                     channel_sums(0, 0, 1)
 
             if s == 1:
@@ -480,8 +484,8 @@ def tile_xmem_pa_t_kernel(
             negated_similarities(s - 1, 1)
             if quarter == 0 and h_now > 0:
                 keep_channel_sums(h_now)
-            if quarter == 3:
-                reciprocals(h_now - 1)
+            if quarter == 0 and h_now - 2 < FINE or quarter == 3 and h_now - 1 == FINE:
+                reciprocals(h_now - (2 if quarter == 0 else 1))
             fine_quantise(s - 6)
             fine_leave(s - 9)
             if s == 6:
@@ -524,15 +528,12 @@ def tile_xmem_pa_t_kernel(
             if s == 1:
                 channel_sums(0, 1)
             similarities(s, 0)
-            if s == 0:
-                spread_shrinkage(1)
             similarities(s, 1)
             turn_e(s - 4)
             if value_tile(s):
                 turn_values(*value_tile(s))
-            if quarter == 0 and h_now - 2 < FINE:
-                spread_reciprocals(h_now - 2, 0)
             if quarter == 1 and h_now - 2 < FINE:
+                spread_reciprocals(h_now - 2, 0)
                 spread_reciprocals(h_now - 2, 1)
             if quarter == 3 and h_now - 1 == FINE:
                 spread_reciprocals(FINE, 0)

@@ -28,7 +28,6 @@ V_TILES = VALUES // P
 TILES = BATCH * ROW_TILES
 HALVES = TILES // HALF_TILES
 V_UNITS = V_TILES * PASSES
-FIRST_SHARED, SHARED_TILES = 5, 10
 FINE = HALVES - 1
 
 FLOPS = 2 * BATCH * (2 * P * SLOTS * PIXELS + VALUES * SLOTS * PIXELS)
@@ -244,7 +243,7 @@ def tile_xmem_pa_t_kernel(
             )
 
         def is_shared(i):
-            return FIRST_SHARED <= i < SHARED_TILES and i % 2 == 1
+            return (5 <= i < 10 and i % 2 == 1) or (25 <= i < TILES and i % 4 == 1)
 
         def shared_similarities(i):
             if not is_shared(i):

import math
from contextlib import ExitStack

import concourse.mybir as mybir
from concourse.masks import make_identity

F32 = mybir.dt.float32
BF16 = mybir.dt.bfloat16
U32 = mybir.dt.uint32
U8 = mybir.dt.uint8
FP8X4 = mybir.dt.float8_e4m3fn_x4
ALU = mybir.AluOpType
ACT = mybir.ActivationFunctionType
AXIS = mybir.AxisListType

BATCH = 4
P = 128
SLOTS = 1024
PIXELS = 1024
VALUES = 512
BANK = 512
PACK = 4
K_PASS = P * PACK
PASSES = SLOTS // K_PASS
ROW_TILES = PIXELS // P
HALF_TILES = BANK // P
V_TILES = VALUES // P
TILES = BATCH * ROW_TILES
HALVES = TILES // HALF_TILES
V_UNITS = V_TILES * PASSES
FINE = HALVES - 1

FLOPS = 2 * BATCH * (2 * P * SLOTS * PIXELS + VALUES * SLOTS * PIXELS)


def tile_xmem_pa_t_kernel(
    tc,
    query_key,
    query_selection,
    qk_sel,
    memory_key,
    mk_sq,
    memory_shrinkage,
    memory_value,
    out,
):
    nc = tc.nc
    with ExitStack() as ctx:
        consts = ctx.enter_context(tc.tile_pool(name="consts", bufs=1))
        inputs = ctx.enter_context(tc.tile_pool(name="inputs", bufs=BATCH))
        prep = ctx.enter_context(tc.tile_pool(name="prep", bufs=2))
        rows = ctx.enter_context(tc.tile_pool(name="rows", bufs=6))
        groups = ctx.enter_context(tc.tile_pool(name="groups", bufs=3))
        halves = ctx.enter_context(tc.tile_pool(name="halves", bufs=2))
        results = ctx.enter_context(tc.tile_pool(name="results", bufs=8))
        psum_wide = ctx.enter_context(tc.psum_pool(name="psum_wide", bufs=4))
        psum_turn = ctx.enter_context(tc.psum_pool(name="psum_turn", bufs=3))
        psum_misc = ctx.enter_context(tc.psum_pool(name="psum_misc", bufs=1))
        ctx.enter_context(tc.manual_schedule())

        live = {}

        first_row = consts.tile([P, P], BF16)
        nc.vector.memset(first_row[:], 0.0)
        nc.vector.memset(first_row[0:1, :], 1.0)
        ms_row = consts.tile([P, SLOTS], BF16)
        nc.gpsimd.memset(ms_row[:].bitcast(U32), 0)

        for b in range(BATCH):
            qk = inputs.tile([P, PIXELS], BF16)
            qe = inputs.tile([P, PIXELS], BF16)
            qs = inputs.tile([P, PIXELS], BF16)
            mk = inputs.tile([P, SLOTS], BF16)
            m2 = inputs.tile([P, SLOTS], BF16)
            mv = inputs.tile([P, V_TILES, SLOTS], BF16)
            qk_hbm = query_key[b].rearrange("c h w -> c (h w)")
            qe_hbm = query_selection[b].rearrange("c h w -> c (h w)")
            qs_hbm = qk_sel[b].rearrange("c h w -> c (h w)")
            mk_hbm = memory_key[b].rearrange("c t h w -> c (t h w)")
            m2_hbm = mk_sq[b].rearrange("c t h w -> c (t h w)")
            mv_hbm = memory_value[b].rearrange("o c t h w -> (o c) (t h w)").rearrange("(j q) n -> q j n", q=P)
            pieces = [slice(0, BANK), slice(BANK, PIXELS)] if b == 0 else [slice(0, PIXELS)]
            nc.sync.dma_start(out=qk[:, pieces[0]], in_=qk_hbm[:, pieces[0]])
            nc.sync.dma_start(out=qe[:, pieces[0]], in_=qe_hbm[:, pieces[0]])
            if b == 0:
                nc.sync.dma_start(out=ms_row[0:1, :], in_=memory_shrinkage[0].rearrange("a t h w -> a (t h w)"))
            nc.sync.dma_start(out=qs[:, pieces[0]], in_=qs_hbm[:, pieces[0]])
            for cols in pieces:
                nc.sync.dma_start(out=mk[:, cols], in_=mk_hbm[:, cols])
                nc.sync.dma_start(out=m2[:, cols], in_=m2_hbm[:, cols])
            if b > 0:
                ms_rows = inputs.tile([P, SLOTS], BF16)
                nc.sync.dma_start(
                    out=ms_rows[:],
                    in_=memory_shrinkage[b].rearrange("a t h w -> (a t h w)").partition_broadcast(P),
                )
                live["ms_rows", b] = ms_rows
            for j in range(0, V_TILES, 2):
                nc.sync.dma_start(out=mv[:, j : j + 2, :], in_=mv_hbm[:, j : j + 2, :])
            for cols in pieces[1:]:
                nc.sync.dma_start(out=qk[:, cols], in_=qk_hbm[:, cols])
                nc.sync.dma_start(out=qe[:, cols], in_=qe_hbm[:, cols])
                nc.sync.dma_start(out=qs[:, cols], in_=qs_hbm[:, cols])
            live["qk", b], live["qe", b], live["qs", b] = qk, qe, qs
            live["mk", b], live["m2", b], live["mv", b] = mk, m2, mv

        ident = consts.tile([P, P], F32)
        make_identity(nc, ident[:])
        ones_column = consts.tile([P, 1], F32)
        nc.gpsimd.memset(ones_column[:], 1.0)

        def square_keys(h, engine, part=slice(0, BANK)):
            b, half = divmod(h, 2)
            if part.start == 0:
                weighted = prep.tile([P, BANK], F32, bufs=3)
                live["weighted", h] = weighted
            keys = live["qk", b][:, half * BANK + part.start : half * BANK + part.stop]
            engine.tensor_tensor(out=live["weighted", h][:, part], in0=keys, in1=keys, op=ALU.mult)

        def weight_squares(h, engine, part=slice(0, BANK)):
            b, half = divmod(h, 2)
            weighted = live["weighted", h][:, part]
            selection = live["qe", b][:, half * BANK + part.start : half * BANK + part.stop]
            engine.tensor_tensor(out=weighted, in0=weighted, in1=selection, op=ALU.mult)

        def scale_queries(b, engine, cols=slice(0, PIXELS)):
            if cols.start == 0:
                qs_scaled = prep.tile([P, PIXELS], BF16)
                live["qs_scaled", b] = qs_scaled
            engine.tensor_scalar(
                out=live["qs_scaled", b][:, cols], in0=live["qs", b][:, cols], scalar1=-2.0, scalar2=0.0,
                op0=ALU.mult, op1=ALU.add,
            )

        def warm_up():
            warm = psum_turn.tile([P, BANK], F32, tag="turned")
            for k in range(14):
                cols = slice(k % HALF_TILES * P, (k % HALF_TILES + 1) * P)
                nc.tensor.matmul(out=warm[:, cols], lhsT=first_row[:], rhs=first_row[:], start=True, stop=True)

        def spread_shrinkage(c):
            if c == 0:
                ms_scaled = prep.tile([P, SLOTS], F32)
                live["ms_scaled", 0] = ms_scaled
            cols = slice(c * BANK, (c + 1) * BANK)
            ms_spread = psum_turn.tile([P, BANK], F32, tag="turned")
            nc.tensor.matmul(out=ms_spread[:], lhsT=first_row[:], rhs=ms_row[:, cols], start=True, stop=True)
            nc.scalar.activation(
                out=live["ms_scaled", 0][:, cols], in_=ms_spread[:], func=ACT.Copy, scale=1.0 / math.sqrt(P)
            )

        def scale_shrinkage(b):
            ms_scaled = prep.tile([P, SLOTS], F32)
            nc.gpsimd.tensor_scalar(
                out=ms_scaled[:], in0=live["ms_rows", b][:], scalar1=1.0 / math.sqrt(P), scalar2=0.0,
                op0=ALU.mult, op1=ALU.add,
            )
            live["ms_scaled", b] = ms_scaled

        def channel_sums(h, first=0, last=HALF_TILES):
            if not 0 <= h < HALVES:
                return
            b_sq_psum = psum_misc.tile([P, HALF_TILES], F32, tag="misc")
            for j in range(first, last):
                nc.tensor.matmul(
                    out=b_sq_psum[:, j : j + 1], lhsT=live["weighted", h][:, j * P : (j + 1) * P],
                    rhs=ones_column[:], start=True, stop=True,
                )
            live["b_sq_psum", h] = b_sq_psum

        def keep_channel_sums(h, first=0, last=HALF_TILES):
            if not 0 <= h < HALVES:
                return
            b_sq = halves.tile([P, HALF_TILES], F32, bufs=3)
            nc.vector.tensor_copy(out=b_sq[:, first:last], in_=live["b_sq_psum", h][:, first:last])
            for j in range(first, last):
                live["b_sq", h, j] = b_sq[:, j : j + 1]

        def turn_words(rows_bf16, turned, first_pass, passes):
            words = rows_bf16.bitcast(F32)
            for k in range(2 * passes):
                g, u = divmod(2 * first_pass + k, 2)
                nc.tensor.transpose(
                    out=turned[:, k, :], in_=words[:, 2 * P * g + u : 2 * P * (g + 1) : 2], identity=ident[:]
                )

        def regroup_words(turned, grouped, passes):
            nc.scalar.copy(
                out=grouped.bitcast(F32).rearrange("q (g r u) -> q g r u", g=passes, u=2),
                in_=turned[:].rearrange("q (g u) r -> q g r u", g=passes),
            )

        def quantise_columns(grouped_cols, codes, scales, cols):
            nc.vector.quantize_mx(out=codes[:, cols].bitcast(FP8X4), scales=scales[:, cols], in_=grouped_cols)

        def turn_values(b, j):
            mv_turned = psum_turn.tile([P, 2 * PASSES, P], F32, tag="turned")
            turn_words(live["mv", b][:, j, :], mv_turned, 0, PASSES)
            live["mv_turned", b, j] = mv_turned

        def regroup_values(b, j):
            if j == 0:
                mv_grouped = groups.tile([P, V_TILES, PASSES * P * PACK], BF16, align_bytes=64, bufs=2)
                live["mv_grouped", b] = mv_grouped
            regroup_words(live["mv_turned", b, j], live["mv_grouped", b][:, j, :], PASSES)

        def quantise_values(b):
            mv_codes = prep.tile([P, V_UNITS * P], U32, align_bytes=64, bufs=3)
            mv_scales = prep.tile([P, V_UNITS * P], U8, align_bytes=64, bufs=3)
            live["mv_codes", b], live["mv_scales", b] = mv_codes, mv_scales
            quantise_columns(
                live["mv_grouped", b][:].rearrange("q k c -> q (k c)"), mv_codes, mv_scales, slice(0, V_UNITS * P)
            )

        def similarities(i, c):
            if not 0 <= i < TILES:
                return
            b, t = divmod(i, ROW_TILES)
            pix = slice(t * P, (t + 1) * P)
            cols = slice(c * BANK, (c + 1) * BANK)
            dots = psum_wide.tile([P, BANK], F32, tag="wide")
            nc.tensor.matmul(
                out=dots[:], lhsT=live["qs_scaled", b][:, pix], rhs=live["mk", b][:, cols], start=True, stop=False
            )
            nc.tensor.matmul(
                out=dots[:], lhsT=live["qe", b][:, pix], rhs=live["m2", b][:, cols], start=False, stop=True
            )
            live["dots", i, c] = dots

        def negated_similarities(i, c):
            if not 0 <= i < TILES:
                return
            h, j = divmod(i, HALF_TILES)
            cols = slice(c * BANK, (c + 1) * BANK)
            if c == 0:
                neg_sim = rows.tile([P, SLOTS], F32)
                live["neg_sim", i] = neg_sim
            if c == 1 and is_shared(i):
                return
            nc.vector.scalar_tensor_tensor(
                out=live["neg_sim", i][:, cols], in0=live["dots", i, c][:], scalar=live["b_sq", h, j],
                in1=live["ms_scaled", i // ROW_TILES][:, cols], op0=ALU.add, op1=ALU.mult,
            )

        def is_shared(i):
            return (5 <= i < 10 and i % 2 == 1) or (25 <= i < TILES and i % 4 == 1)

        def shared_similarities(i):
            if not is_shared(i):
                return
            h, j = divmod(i, HALF_TILES)
            cols = slice(BANK, SLOTS)
            neg_sim = live["neg_sim", i]
            nc.scalar.activation(
                out=neg_sim[:, cols], in_=live["dots", i, 1][:], func=ACT.Identity, bias=live["b_sq", h, j], scale=1.0
            )
            nc.gpsimd.tensor_tensor(
                out=neg_sim[:, cols], in0=neg_sim[:, cols], in1=live["ms_scaled", i // ROW_TILES][:, cols], op=ALU.mult
            )

        def negated_maximum(i):
            if not 0 <= i < TILES:
                return
            neg_max = rows.tile([P, 1], F32)
            nc.vector.tensor_reduce(out=neg_max[:], in_=live["neg_sim", i][:], axis=AXIS.X, op=ALU.min)
            live["neg_max", i] = neg_max

        def exponentials(i):
            if not 0 <= i < TILES:
                return
            h, j = divmod(i, HALF_TILES)
            if j == 0:
                sums = halves.tile([P, HALF_TILES], F32)
                live["sums", h] = sums
            e_rows = rows.tile([P, SLOTS], BF16)
            nc.scalar.activation(
                out=e_rows[:], in_=live["neg_sim", i][:], func=ACT.Exp, bias=live["neg_max", i][:], scale=-1.0,
                accum_out=live["sums", h][:, j : j + 1],
            )
            live["e_rows", i] = e_rows

        def turn_e(i):
            if not 0 <= i < TILES:
                return
            e_turned = psum_turn.tile([P, 2 * PASSES, P], F32, tag="turned")
            turn_words(live["e_rows", i][:], e_turned, 0, PASSES)
            live["e_turned", i] = e_turned

        def regroup_e(i):
            if not 0 <= i < TILES:
                return
            h, j = divmod(i, HALF_TILES)
            if h == FINE:
                e_fine = halves.tile([P, PASSES, P, PACK], BF16, align_bytes=64, bufs=HALF_TILES)
                live["e_fine", i] = e_fine
                target = e_fine[:].bitcast(F32)
            else:
                if j == 0:
                    e_grouped = halves.tile([P, PASSES, BANK, PACK], BF16, align_bytes=64)
                    live["e_grouped", h] = e_grouped
                target = live["e_grouped", h][:].bitcast(F32)[:, :, j * P : (j + 1) * P, :]
            nc.scalar.copy(
                out=target, in_=live["e_turned", i][:].rearrange("q (g u) r -> q g r u", g=PASSES)
            )

        def quantise_e(h):
            if not 0 <= h < FINE:
                return
            e_codes = halves.tile([P, PASSES * BANK], U32, align_bytes=64)
            e_scales = halves.tile([P, PASSES * BANK], U8, align_bytes=64)
            quantise_columns(
                live["e_grouped", h][:].rearrange("q g r t -> q (g r t)"), e_codes, e_scales, slice(0, PASSES * BANK)
            )
            live["e_codes", h], live["e_scales", h] = e_codes, e_scales

        def is_fine(i):
            return FINE * HALF_TILES <= i < TILES

        def fine_quantise(i):
            if not is_fine(i):
                return
            fine_codes = halves.tile([P, PASSES * P], U32, align_bytes=64, bufs=HALF_TILES)
            fine_scales = halves.tile([P, PASSES * P], U8, align_bytes=64, bufs=HALF_TILES)
            quantise_columns(
                live["e_fine", i][:].rearrange("q g r t -> q (g r t)"), fine_codes, fine_scales, slice(0, PASSES * P)
            )
            live["fine_codes", i], live["fine_scales", i] = fine_codes, fine_scales

        def fine_multiply(i):
            if not is_fine(i):
                return
            b = i // ROW_TILES
            fine_acc = psum_wide.tile([P, V_TILES, P], F32, tag="wide")
            for j in range(V_TILES):
                for g in range(PASSES):
                    v_cols = slice((j * PASSES + g) * P, (j * PASSES + g + 1) * P)
                    p_cols = slice(g * P, (g + 1) * P)
                    nc.tensor.matmul_mx(
                        out=fine_acc[:, j, :],
                        lhsT=live["mv_codes", b][:, v_cols].bitcast(FP8X4),
                        lhsT_scale=live["mv_scales", b][:, v_cols],
                        rhs=live["fine_codes", i][:, p_cols].bitcast(FP8X4),
                        rhs_scale=live["fine_scales", i][:, p_cols],
                        start=(g == 0),
                        stop=(g == PASSES - 1),
                    )
            live["fine_acc", i] = fine_acc

        def fine_leave(i):
            if not is_fine(i):
                return
            b, t = divmod(i, ROW_TILES)
            h, j = divmod(i, HALF_TILES)
            fine_result = results.tile([P, V_TILES, P], F32, bufs=HALF_TILES)
            step = V_TILES // 2 if i == TILES - 1 else V_TILES
            for a in range(0, V_TILES, step):
                channels = slice(a, a + step)
                nc.vector.tensor_tensor(
                    out=fine_result[:, channels, :], in0=live["fine_acc", i][:, channels, :],
                    in1=live["recip_rows", h][:, j * P : (j + 1) * P].unsqueeze(1).to_broadcast([P, step, P]), op=ALU.mult,
                )
                nc.sync.dma_start(
                    out=out[b].rearrange("o c h w -> (o c) (h w)").rearrange("(j q) p -> q j p", q=P)[
                        :, channels, t * P : (t + 1) * P
                    ],
                    in_=fine_result[:, channels, :],
                )

        def reciprocals(h):
            if not 0 <= h < HALVES:
                return
            recip = halves.tile([P, HALF_TILES], F32)
            nc.vector.reciprocal(out=recip[:], in_=live["sums", h][:])
            live["recip", h] = recip

        def spread_reciprocals(h, part):
            if not 0 <= h < HALVES:
                return
            if part == 0:
                recip_spread = psum_misc.tile([P, BANK], F32, tag="misc")
                live["recip_spread", h] = recip_spread
            for j in (2 * part, 2 * part + 1):
                nc.tensor.transpose(
                    out=live["recip_spread", h][:, j * P : (j + 1) * P],
                    in_=live["recip", h][:, j : j + 1].to_broadcast([P, P]),
                    identity=ident[:],
                )

        def keep_reciprocals(h):
            if not 0 <= h < HALVES:
                return
            recip_rows = halves.tile([P, BANK], F32)
            nc.scalar.copy(out=recip_rows[:], in_=live["recip_spread", h][:])
            live["recip_rows", h] = recip_rows

        def multiply_values(h, j):
            if not 0 <= h < FINE:
                return
            b = h // 2
            acc = psum_wide.tile([P, BANK], F32, tag="wide")
            for g in range(PASSES):
                v_cols = slice((j * PASSES + g) * P, (j * PASSES + g + 1) * P)
                p_cols = slice(g * BANK, (g + 1) * BANK)
                nc.tensor.matmul_mx(
                    out=acc[:],
                    lhsT=live["mv_codes", b][:, v_cols].bitcast(FP8X4),
                    lhsT_scale=live["mv_scales", b][:, v_cols],
                    rhs=live["e_codes", h][:, p_cols].bitcast(FP8X4),
                    rhs_scale=live["e_scales", h][:, p_cols],
                    start=(g == 0),
                    stop=(g == PASSES - 1),
                )
            live["acc", h, j] = acc

        def store(h, j, result):
            b, half = divmod(h, 2)
            nc.sync.dma_start(
                out=out[b].rearrange("o c h w -> (o c) (h w)")[
                    j * P : (j + 1) * P, half * BANK : (half + 1) * BANK
                ],
                in_=result[:],
            )

        def on_vector(h, j):
            return h >= FINE - 1 or (h == FINE - 2 and j >= 2)

        def leave_psum(h, j):
            if not 0 <= h < FINE:
                return
            result = results.tile([P, BANK], F32)
            if not on_vector(h, j):
                nc.scalar.copy(out=result[:], in_=live["acc", h, j][:])
                live["result", h, j] = result
            else:
                nc.vector.tensor_tensor(
                    out=result[:], in0=live["acc", h, j][:], in1=live["recip_rows", h][:], op=ALU.mult
                )
                store(h, j, result)

        def normalise_and_store(h, j):
            if not 0 <= h < HALVES or on_vector(h, j):
                return
            result = live["result", h, j]
            nc.gpsimd.tensor_tensor(out=result[:], in0=result[:], in1=live["recip_rows", h][:], op=ALU.mult)
            store(h, j, result)

        def value_tile(s):
            if 1 <= s <= 2 * V_TILES:
                return divmod(s - 1, V_TILES)
            if 2 * V_TILES < s <= (BATCH - 1) * V_UNITS and s % 2 == 0:
                return 2 + (s - 10) // V_UNITS, (s - 10) % V_UNITS // 2
            return None

        for s in range(-ROW_TILES, TILES + 14):
            b_next, step = divmod(s + ROW_TILES, ROW_TILES)
            h_now, quarter = divmod(s, HALF_TILES)

            if b_next == 0:
                first, pixels = slice(0, BANK), (slice(0, P), slice(P, BANK))
                if step == 0:
                    square_keys(0, nc.vector, pixels[0])
                    weight_squares(0, nc.vector, pixels[0])
                    scale_queries(0, nc.vector, first)
                    square_keys(0, nc.vector, pixels[1])
                    weight_squares(0, nc.vector, pixels[1])
                    warm_up()
                if step == 1:
                    spread_shrinkage(0)
                    spread_shrinkage(1)
                    channel_sums(0, 0, 1)

            if s == 1:
                keep_channel_sums(0, 0, 1)
            if s == 2:
                keep_channel_sums(0, 1)
            if s == 2:
                negated_maximum(0)
            negated_similarities(s - 1, 0)
            if s > 2:
                negated_maximum(s - 2)
            if quarter == 1:
                quantise_e(h_now - 2)
            negated_similarities(s - 1, 1)
            if quarter == 0 and h_now > 0:
                keep_channel_sums(h_now)
            if quarter == 0 and h_now - 2 < FINE or quarter == 3 and h_now - 1 == FINE:
                reciprocals(h_now - (2 if quarter == 0 else 1))
            fine_quantise(s - 6)
            fine_leave(s - 9)
            if s == 6:
                quantise_values(0)
            if s % V_UNITS == V_UNITS - 1 and V_UNITS < s < TILES:
                quantise_values(s // V_UNITS)

            shared_similarities(s - 1)
            exponentials(s - 3)
            if quarter == 2 and h_now - 2 < FINE:
                keep_reciprocals(h_now - 2)
            regroup_e(s - 5)
            if quarter == 0 and h_now - 2 == FINE:
                keep_reciprocals(FINE)
            if value_tile(s - 1):
                regroup_values(*value_tile(s - 1))
            leave_psum((s - 11) // V_TILES, (s - 11) % V_TILES)

            if s == 1:
                square_keys(1, nc.gpsimd)
                weight_squares(1, nc.gpsimd)
            if s == 2:
                scale_queries(0, nc.gpsimd, slice(BANK, PIXELS))
            if 0 < b_next < BATCH:
                if step == 2:
                    square_keys(2 * b_next, nc.gpsimd)
                if step == 3:
                    weight_squares(2 * b_next, nc.gpsimd)
                if step == 4:
                    scale_queries(b_next, nc.gpsimd)
                if step == 5:
                    scale_shrinkage(b_next)
                if step == 6:
                    square_keys(2 * b_next + 1, nc.gpsimd)
                if step == 7:
                    weight_squares(2 * b_next + 1, nc.gpsimd)
            normalise_and_store((s - 12) // V_TILES, (s - 12) % V_TILES)


            if s == 1:
                channel_sums(0, 1)
            similarities(s, 0)
            similarities(s, 1)
            turn_e(s - 4)
            if value_tile(s):
                turn_values(*value_tile(s))
            if quarter == 1 and h_now - 2 < FINE:
                spread_reciprocals(h_now - 2, 0)
                spread_reciprocals(h_now - 2, 1)
            if quarter == 3 and h_now - 1 == FINE:
                spread_reciprocals(FINE, 0)
                spread_reciprocals(FINE, 1)
            if quarter == 3 and h_now + 1 > 0:
                channel_sums(h_now + 1)
            multiply_values((s - 10) // V_TILES, (s - 10) % V_TILES)
            fine_multiply(s - 7)
